import numpy as np
import ml_dtypes


def mxq(x, axis, fmt="e4m3"):
    dtype, down = {"e4m3": (ml_dtypes.float8_e4m3fn, 7), "e5m2": (ml_dtypes.float8_e5m2, 14)}[fmt]
    v = np.moveaxis(np.asarray(x, np.float32).astype(ml_dtypes.bfloat16).astype(np.float64), axis, -1)
    blocks = v.reshape(v.shape[:-1] + (-1, 32))
    amax = np.abs(blocks).max(-1, keepdims=True)
    byte = np.maximum(np.where(amax > 0, np.frexp(amax)[1] - 1 + 127, 0) - down, 1)
    scale = np.exp2(byte - 127.0)
    codes = (blocks / scale).astype(np.float32).astype(dtype).astype(np.float64)
    return np.moveaxis((codes * scale).reshape(v.shape), -1, axis)


WIDE = False


def mx_kscale(k):
    if not WIDE:
        return np.ones(k)
    levels = np.array([10, -10, 5, -5, 0])
    a = np.random.permutation(np.resize(levels, k // 512 * 4)).reshape(k // 512, 4)
    idx = np.arange(k)
    return np.exp2(a[idx // 512, idx % 128 // 32])


BF16 = ml_dtypes.bfloat16


def bf(x):
    return np.asarray(x, np.float32).astype(BF16)


def f64(x):
    return np.asarray(x).astype(np.float64)


NX, NTEST, DX, DY = 2048, 1024, 256, 256
L_VAR = 8.0
DV = DX + 2 * DY
SIGV = 2.0 * L_VAR / np.sqrt(DV)
SIGY = L_VAR / np.sqrt(DX + DY)
ZS = np.exp(4.0) / np.sqrt(NX)


def setup_inputs():
    s = mx_kscale(NX)
    return {"x_var": bf(np.random.standard_normal((NTEST, DV)) * SIGV),
            "X_var": bf(np.random.standard_normal((NX, DV)) * SIGV),
            "Z_var": bf(np.random.standard_normal((NX, DY)) * ZS / s[:, None]),
            "kXXvar_inv": bf(np.random.standard_normal((NX, NX)) / np.sqrt(NX) * s),
            "y_var": bf(np.random.standard_normal((NTEST, DY)) * SIGY),
            "h_mean": bf(np.random.standard_normal((NTEST, DY)))}


def reference(x_var, X_var, Z_var, kXXvar_inv, y_var, h_mean):
    lam = mxq(f64(kXXvar_inv), 1, "e4m3") @ mxq(f64(Z_var), 0, "e4m3")
    d2 = (np.sum(f64(X_var) * f64(X_var), axis=1)[:, None]
          + np.sum(f64(x_var) * f64(x_var), axis=1)[None, :]
          - 2.0 * (f64(X_var) @ f64(x_var).T))
    k = np.exp(-np.maximum(d2, 0.0) / (2.0 * L_VAR * L_VAR))
    z_var = mxq(k, 0, "e4m3").T @ mxq(lam, 0, "e4m3")
    return f64(h_mean) + (f64(y_var) + z_var)

@@ -1,0 +1,386 @@
+from contextlib import ExitStack
+
+import concourse.mybir as mybir
+from concourse.masks import make_identity
+
+F32 = mybir.dt.float32
+BF16 = mybir.dt.bfloat16
+U32 = mybir.dt.uint32
+U8 = mybir.dt.uint8
+FP8X4 = mybir.dt.float8_e4m3fn_x4
+ALU = mybir.AluOpType
+ACT = mybir.ActivationFunctionType
+
+P = 128
+NX, NT, DV, DY = 2048, 1024, 768, 256
+BANK = 512
+PASS = 4 * P
+GROUPS = NX // PASS
+I_TILES = NX // P
+HALVES = NT // BANK
+ROW_WORDS = DV // 2
+CW = ROW_WORDS // P
+UNIT_MATMULS = 2 * CW
+ROUNDS = I_TILES
+ROUND_MATMULS = 2 * UNIT_MATMULS
+LAM_LAG = 2
+KIN_BUFS = 4
+
+FLOPS = 2 * NX * NX * DY + 2 * NX * NT * DV + 2 * NT * NX * DY
+
+
+def tile_condtransportkernel_pb_kernel(
+    tc, x_var, X_var, Z_var, kXXvar_inv, y_var, h_mean, out
+):
+    nc = tc.nc
+    x_rows = x_var.rearrange("(h q p) c -> h p q c", h=HALVES, p=P)
+    X_rows = X_var.rearrange("(g q p) c -> g p q c", g=GROUPS, p=P)
+    kin_rows = kXXvar_inv.rearrange("(i p) j -> i p j", p=P)
+    Z_rows = Z_var.rearrange("(a q e) d -> q a (e d)", q=P, e=2)
+    y_rows = y_var.rearrange("(a p) d -> p a d", p=P)
+    h_rows = h_mean.rearrange("(a p) d -> p a d", p=P)
+    out_rows = out.rearrange("(a p) d -> p a d", p=P)
+
+    with ExitStack() as ctx:
+        keep = ctx.enter_context(tc.tile_pool(name="keep", bufs=1))
+        ring = ctx.enter_context(tc.tile_pool(name="ring", bufs=2))
+        psum = ctx.enter_context(tc.psum_pool(name="psum", bufs=2))
+        ctx.enter_context(tc.manual_schedule())
+
+        ident = keep.tile([P, P], F32, name="ident")
+        half_ident = keep.tile([P, P], F32, name="half_ident")
+        zero_col = keep.tile([P, 1], F32, name="zero_col")
+        one_col = keep.tile([P, 1], F32, name="one_col")
+        x_sq = keep.tile([P, NT // P], F32, name="x_sq")
+        X_sq = keep.tile([P, I_TILES], F32, name="X_sq")
+        X_sq_half = keep.tile([P, I_TILES], F32, name="X_sq_half")
+        x_sq_half_all = keep.tile([P, NT], F32, name="x_sq_half_all")
+        x_raw = [keep.tile([P, 4 * DV], BF16, name="x_raw%d" % h) for h in range(HALVES)]
+        xT = keep.tile([P, CW * NT], F32, name="xT")
+        z_raw = keep.tile([P, GROUPS * 4 * DY], BF16, name="z_raw")
+        z_grouped = keep.tile([P, GROUPS * DY * 4], BF16, name="z_grouped", align_bytes=64)
+        z_codes = keep.tile([P, GROUPS * DY], U32, name="z_codes", align_bytes=64)
+        z_scales = keep.tile([P, GROUPS * DY], U8, name="z_scales", align_bytes=64)
+        kin_codes = keep.tile([P, I_TILES * PASS], U32, name="kin_codes", align_bytes=64)
+        kin_scales = keep.tile([P, I_TILES * PASS], U8, name="kin_scales", align_bytes=64)
+        k_codes = keep.tile([P, GROUPS * NT], U32, name="k_codes", align_bytes=64)
+        k_scales = keep.tile([P, GROUPS * NT], U8, name="k_scales", align_bytes=64)
+        lam_codes = keep.tile([P, GROUPS * DY], U32, name="lam_codes", align_bytes=64)
+        lam_scales = keep.tile([P, GROUPS * DY], U8, name="lam_scales", align_bytes=64)
+        y_raw = keep.tile([P, NT // P * DY], BF16, name="y_raw")
+        h_raw = keep.tile([P, NT // P * DY], BF16, name="h_raw")
+        partial = keep.tile([P, NT // P * DY], F32, name="partial")
+
+        xT_pairs = xT[:].bitcast(BF16).rearrange("p (w t e) -> p w t e", w=CW, e=2)
+        X_raw = {}
+        XT = {}
+        kin_raw = {}
+        kin_grouped = {}
+        k_rows = {}
+        k_grouped = {}
+        lam_rows = {}
+        lam_grouped = {}
+        tr_bank = {}
+
+        def load_X(g):
+            X_raw[g] = ring.tile([P, 4 * DV], BF16, name="X_raw", tag="X_raw", bufs=2)
+            nc.sync.dma_start(
+                out=X_raw[g][:].rearrange("p (q c) -> p q c", q=4), in_=X_rows[g]
+            )
+
+        def load_kin(it):
+            kin_raw[it] = ring.tile([P, NX], BF16, name="kin_raw", tag="kin_raw", bufs=KIN_BUFS)
+            nc.sync.dma_start(out=kin_raw[it][:], in_=kin_rows[it])
+
+        def new_transpose_bank():
+            return psum.tile([P, BANK], F32, name="tr", tag="tr", bufs=3)
+
+        def transpose_words(bank, pos, raw, first_word):
+            nc.tensor.transpose(
+                out=bank[:, pos * P : (pos + 1) * P],
+                in_=raw[:].bitcast(F32)[:, first_word : first_word + P],
+                identity=ident[:],
+            )
+
+        def sum_of_squares(rows, q, result_column):
+            squares = ring.tile([P, DV], BF16, name="squares", tag="squares", bufs=2)
+            nc.scalar.activation(
+                out=squares[:],
+                in_=rows[:, q * DV : (q + 1) * DV],
+                func=ACT.Square,
+                accum_out=result_column,
+            )
+
+        def spread_query_norms(th):
+            bank = new_transpose_bank()
+            for q in range(4):
+                tile_col = 4 * th + q
+                nc.tensor.matmul(
+                    out=bank[:, q * P : (q + 1) * P],
+                    lhsT=x_sq[:, tile_col : tile_col + 1].to_broadcast([P, P]),
+                    rhs=half_ident[:],
+                    start=True,
+                    stop=True,
+                )
+            nc.vector.tensor_copy(out=x_sq_half_all[:, th * BANK : (th + 1) * BANK], in_=bank[:])
+
+        make_identity(nc, ident[:])
+        nc.vector.memset(zero_col[:], 0.0)
+        nc.scalar.activation(out=one_col[:], in_=zero_col[:], func=ACT.Exp)
+        nc.vector.tensor_scalar_mul(out=half_ident[:], in0=ident[:], scalar1=0.5)
+
+        for h in range(HALVES):
+            nc.sync.dma_start(
+                out=x_raw[h][:].rearrange("p (q c) -> p q c", q=4), in_=x_rows[h]
+            )
+        load_X(0)
+        load_kin(0)
+        nc.sync.dma_start(out=z_raw[:].rearrange("p (a r) -> p a r", r=2 * DY), in_=Z_rows)
+        load_X(1)
+        for it in range(1, KIN_BUFS - 1):
+            load_kin(it)
+
+        for h in range(HALVES):
+            for cw in range(CW):
+                bank = new_transpose_bank()
+                for q in range(4):
+                    transpose_words(bank, q, x_raw[h], q * ROW_WORDS + cw * P)
+                nc.vector.tensor_copy(
+                    out=xT[:, cw * NT + h * BANK : cw * NT + (h + 1) * BANK], in_=bank[:]
+                )
+        XT[0] = ring.tile([P, CW * PASS], F32, name="XT", tag="XT", bufs=2)
+        for cw in range(CW):
+            bank = new_transpose_bank()
+            for q in range(4):
+                transpose_words(bank, q, X_raw[0], q * ROW_WORDS + cw * P)
+            nc.vector.tensor_copy(out=XT[0][:, cw * PASS : (cw + 1) * PASS], in_=bank[:])
+        for q in range(4):
+            sum_of_squares(x_raw[0], q, x_sq[:, q : q + 1])
+        for q in range(4):
+            sum_of_squares(X_raw[0], q, X_sq[:, q : q + 1])
+        nc.vector.tensor_scalar_mul(out=X_sq_half[:, 0:4], in0=X_sq[:, 0:4], scalar1=0.5)
+        for q in range(4):
+            sum_of_squares(x_raw[1], q, x_sq[:, 4 + q : 5 + q])
+
+        z_by_column = z_raw[:].rearrange("p (g t d) -> p g d t", g=GROUPS, t=4)
+        z_words = z_grouped[:].rearrange("p (g d t) -> p g d t", g=GROUPS, t=4)
+        for g in range(GROUPS):
+            nc.gpsimd.tensor_scalar(
+                out=z_words[:, g], in0=z_by_column[:, g], scalar1=1.0, scalar2=0.0,
+                op0=ALU.mult, op1=ALU.add,
+            )
+
+        def weave(r, m):
+            g_next = r // 4 + 1
+            jobs = [("kin", 0), ("kin", 1)]
+            if r % 4 >= 1 and g_next < GROUPS:
+                jobs = [("X", r % 4 - 1)] + jobs
+            b, pos = divmod(m, 4)
+            if b >= len(jobs):
+                return
+            kind, part = jobs[b]
+            if pos == 0:
+                tr_bank[b] = new_transpose_bank()
+            bank = tr_bank[b]
+            if kind == "X":
+                transpose_words(bank, pos, X_raw[g_next], pos * ROW_WORDS + part * P)
+                if pos == 3:
+                    if part == 0:
+                        XT[g_next] = ring.tile([P, CW * PASS], F32, name="XT", tag="XT", bufs=2)
+                    nc.vector.tensor_copy(
+                        out=XT[g_next][:, part * PASS : (part + 1) * PASS], in_=bank[:]
+                    )
+            else:
+                transpose_words(bank, pos, kin_raw[r], part * BANK + pos * P)
+                if pos == 3:
+                    if part == 0:
+                        kin_grouped[r] = ring.tile(
+                            [P, NX // 2], F32, name="kin_grouped", tag="kin_grouped", bufs=2,
+                            align_bytes=64,
+                        )
+                    nc.scalar.copy(
+                        out=kin_grouped[r][:].rearrange("p (g i u) -> p g i u", g=GROUPS, u=2)[
+                            :, 2 * part : 2 * part + 2
+                        ],
+                        in_=bank[:].rearrange("p (b u i) -> p b i u", b=2, u=2),
+                    )
+
+        def gram_unit(r, unit):
+            n = 2 * r + unit
+            g, th, j = n // 8, (n % 8) // 4, n % 4
+            X_pairs = XT[g][:].bitcast(BF16).rearrange("p (w i e) -> p w i e", w=CW, e=2)
+            gram = psum.tile([P, BANK], F32, name="gram", tag="gram", bufs=3)
+            for kc in range(UNIT_MATMULS):
+                cw, e = divmod(kc, 2)
+                nc.tensor.matmul(
+                    out=gram[:],
+                    lhsT=X_pairs[:, cw, j * P : (j + 1) * P, e],
+                    rhs=xT_pairs[:, cw, th * BANK : (th + 1) * BANK, e],
+                    start=(kc == 0),
+                    stop=(kc == UNIT_MATMULS - 1),
+                )
+                weave(r, unit * UNIT_MATMULS + kc)
+            if g == 0 and j == 0:
+                spread_query_norms(th)
+            minus_half_d2 = ring.tile([P, BANK], F32, name="minus_half_d2", tag="mhd2", bufs=3)
+            nc.vector.scalar_tensor_tensor(
+                out=minus_half_d2[:],
+                in0=gram[:],
+                scalar=X_sq_half[:, 4 * g + j : 4 * g + j + 1],
+                in1=x_sq_half_all[:, th * BANK : (th + 1) * BANK],
+                op0=ALU.subtract,
+                op1=ALU.subtract,
+            )
+            if j == 0:
+                k_rows[(g, th)] = ring.tile([P, 4 * BANK], BF16, name="k_rows", tag="k_rows", bufs=2)
+            nc.scalar.activation(
+                out=k_rows[(g, th)][:, j * BANK : (j + 1) * BANK],
+                in_=minus_half_d2[:],
+                func=ACT.Exp,
+                scale=1.0 / 64.0,
+            )
+
+        def quantise_kin(it):
+            nc.vector.quantize_mx(
+                out=kin_codes[:, it * PASS : (it + 1) * PASS].bitcast(FP8X4),
+                scales=kin_scales[:, it * PASS : (it + 1) * PASS],
+                in_=kin_grouped[it][:].bitcast(BF16),
+            )
+
+        def lam_tile(it):
+            g, j = divmod(it, 4)
+            acc = psum.tile([P, BANK], F32, name="mx", tag="mx", bufs=2)
+            for c in range(GROUPS):
+                nc.tensor.matmul_mx(
+                    out=acc[:, 0:DY],
+                    lhsT=kin_codes[:, it * PASS + c * P : it * PASS + (c + 1) * P].bitcast(FP8X4),
+                    lhsT_scale=kin_scales[:, it * PASS + c * P : it * PASS + (c + 1) * P],
+                    rhs=z_codes[:, c * DY : (c + 1) * DY].bitcast(FP8X4),
+                    rhs_scale=z_scales[:, c * DY : (c + 1) * DY],
+                    start=(c == 0),
+                    stop=(c == GROUPS - 1),
+                )
+            if j == 0:
+                lam_rows[g] = ring.tile([P, 4 * DY], BF16, name="lam_rows", tag="lam_rows", bufs=2)
+            nc.scalar.copy(out=lam_rows[g][:, j * DY : (j + 1) * DY], in_=acc[:, 0:DY])
+
+        def k_block(r):
+            quad, side = r // 2 - 1, r % 2
+            g, th = divmod(quad, HALVES)
+            return g, th, side * (BANK // 2)
+
+        def regroup_k(r):
+            g, th, first = k_block(r)
+            k_grouped[r] = ring.tile(
+                [P, 2 * BANK], BF16, name="k_grouped", tag="k_grouped", bufs=2, align_bytes=64
+            )
+            nc.vector.tensor_scalar_min(
+                out=k_grouped[r][:].rearrange("p (w j) -> p w j", j=4),
+                in0=k_rows[(g, th)][:].rearrange("p (j w) -> p w j", j=4)[
+                    :, first : first + BANK // 2
+                ],
+                scalar1=1.0,
+            )
+
+        def quantise_k(r):
+            g, th, first = k_block(r)
+            col = g * NT + th * BANK + first
+            nc.vector.quantize_mx(
+                out=k_codes[:, col : col + BANK // 2].bitcast(FP8X4),
+                scales=k_scales[:, col : col + BANK // 2],
+                in_=k_grouped[r][:],
+            )
+
+        def regroup_lam(g):
+            lam_grouped[g] = ring.tile(
+                [P, 4 * DY], BF16, name="lam_grouped", tag="lam_grouped", bufs=2, align_bytes=64
+            )
+            nc.vector.tensor_copy(
+                out=lam_grouped[g][:].rearrange("p (d j) -> p d j", j=4),
+                in_=lam_rows[g][:].rearrange("p (j d) -> p d j", j=4),
+            )
+
+        def quantise_lam(g):
+            nc.vector.quantize_mx(
+                out=lam_codes[:, g * DY : (g + 1) * DY].bitcast(FP8X4),
+                scales=lam_scales[:, g * DY : (g + 1) * DY],
+                in_=lam_grouped[g][:],
+            )
+
+        def regression_passes(pair, groups):
+            acc = psum.tile([P, BANK], F32, name="mx", tag="mx", bufs=2)
+            for s in range(2):
+                t0 = (2 * pair + s) * P
+                for g in groups:
+                    nc.tensor.matmul_mx(
+                        out=acc[:, s * DY : (s + 1) * DY],
+                        lhsT=k_codes[:, g * NT + t0 : g * NT + t0 + P].bitcast(FP8X4),
+                        lhsT_scale=k_scales[:, g * NT + t0 : g * NT + t0 + P],
+                        rhs=lam_codes[:, g * DY : (g + 1) * DY].bitcast(FP8X4),
+                        rhs_scale=lam_scales[:, g * DY : (g + 1) * DY],
+                        start=(g == groups[0]),
+                        stop=(g == groups[-1]),
+                    )
+            return acc
+
+        early_groups = list(range(GROUPS - 1))
+        for r in range(ROUNDS + LAM_LAG):
+            g_next = r // 4 + 1
+            if r + KIN_BUFS - 1 < I_TILES:
+                load_kin(r + KIN_BUFS - 1)
+            if r % 4 == 2 and g_next + 1 < GROUPS:
+                load_X(g_next + 1)
+            if r == 4:
+                nc.sync.dma_start(out=y_raw[:].rearrange("p (a d) -> p a d", d=DY), in_=y_rows)
+                nc.sync.dma_start(out=h_raw[:].rearrange("p (a d) -> p a d", d=DY), in_=h_rows)
+                nc.gpsimd.tensor_tensor(out=partial[:], in0=y_raw[:], in1=h_raw[:], op=ALU.add)
+            if r >= LAM_LAG:
+                lam_tile(r - LAM_LAG)
+
+            if r < ROUNDS:
+                gram_unit(r, 0)
+            if r == 1:
+                nc.vector.quantize_mx(
+                    out=z_codes[:].bitcast(FP8X4), scales=z_scales[:], in_=z_grouped[:]
+                )
+            if 1 <= r <= ROUNDS:
+                quantise_kin(r - 1)
+            if r >= 2:
+                regroup_k(r)
+            if r < ROUNDS and g_next < GROUPS:
+                col = 4 * g_next + r % 4
+                sum_of_squares(X_raw[g_next], r % 4, X_sq[:, col : col + 1])
+            if ROUNDS - 2 <= r < ROUNDS:
+                for pair in (2 * (r - ROUNDS + 2), 2 * (r - ROUNDS + 2) + 1):
+                    acc = regression_passes(pair, early_groups)
+                    cols = slice(pair * BANK, (pair + 1) * BANK)
+                    nc.vector.tensor_tensor(
+                        out=partial[:, cols], in0=acc[:], in1=partial[:, cols], op=ALU.add
+                    )
+
+            if r < ROUNDS:
+                gram_unit(r, 1)
+            lam_group_done = r >= LAM_LAG and (r - LAM_LAG) % 4 == 3
+            if lam_group_done:
+                regroup_lam((r - LAM_LAG) // 4)
+            if r >= 2:
+                quantise_k(r)
+            if lam_group_done:
+                quantise_lam((r - LAM_LAG) // 4)
+            if r % 4 == 3 and g_next < GROUPS:
+                nc.vector.tensor_scalar_mul(
+                    out=X_sq_half[:, 4 * g_next : 4 * g_next + 4],
+                    in0=X_sq[:, 4 * g_next : 4 * g_next + 4],
+                    scalar1=0.5,
+                )
+
+        for pair in range(NT // P // 2):
+            acc = regression_passes(pair, [GROUPS - 1])
+            result = ring.tile([P, BANK], F32, name="result", tag="result", bufs=2)
+            nc.vector.tensor_tensor(
+                out=result[:], in0=acc[:], in1=partial[:, pair * BANK : (pair + 1) * BANK], op=ALU.add
+            )
+            nc.sync.dma_start(
+                out=out_rows[:, 2 * pair : 2 * pair + 2, :],
+                in_=result[:].rearrange("p (a d) -> p a d", d=DY),
+            )

@@ -17,14 +17,17 @@ BANK = 512
 PASS = 4 * P
 GROUPS = NX // PASS
 I_TILES = NX // P
+T_TILES = NT // P
 HALVES = NT // BANK
 ROW_WORDS = DV // 2
 CW = ROW_WORDS // P
 UNIT_MATMULS = 2 * CW
-ROUNDS = I_TILES
-ROUND_MATMULS = 2 * UNIT_MATMULS
-LAM_LAG = 2
-KIN_BUFS = 4
+UNITS = I_TILES * HALVES
+PIECE = BANK // 2
+KIN_BUFS = 6
+QUANTISE_LAG = 1
+LAM_LAG = 3
+Z_UNIT = 8
 
 FLOPS = 2 * NX * NX * DY + 2 * NX * NT * DV + 2 * NT * NX * DY
 
@@ -33,7 +36,8 @@ def tile_condtransportkernel_pb_kernel(
     tc, x_var, X_var, Z_var, kXXvar_inv, y_var, h_mean, out
 ):
     nc = tc.nc
-    x_rows = x_var.rearrange("(h q p) c -> h p q c", h=HALVES, p=P)
+    x_tiles = x_var.rearrange("(a p) c -> a p c", p=P)
+    x_halves = x_var.rearrange("(h q p) c -> h p q c", h=HALVES, p=P)
     X_rows = X_var.rearrange("(g q p) c -> g p q c", g=GROUPS, p=P)
     kin_rows = kXXvar_inv.rearrange("(i p) j -> i p j", p=P)
     Z_rows = Z_var.rearrange("(a q e) d -> q a (e d)", q=P, e=2)
@@ -48,44 +52,51 @@ def tile_condtransportkernel_pb_kernel(
         ctx.enter_context(tc.manual_schedule())
 
         ident = keep.tile([P, P], F32, name="ident")
-        half_ident = keep.tile([P, P], F32, name="half_ident")
         zero_col = keep.tile([P, 1], F32, name="zero_col")
         one_col = keep.tile([P, 1], F32, name="one_col")
-        x_sq = keep.tile([P, NT // P], F32, name="x_sq")
-        X_sq = keep.tile([P, I_TILES], F32, name="X_sq")
+        x_sq_half = keep.tile([P, T_TILES], F32, name="x_sq_half")
         X_sq_half = keep.tile([P, I_TILES], F32, name="X_sq_half")
         x_sq_half_all = keep.tile([P, NT], F32, name="x_sq_half_all")
-        x_raw = [keep.tile([P, 4 * DV], BF16, name="x_raw%d" % h) for h in range(HALVES)]
-        xT = keep.tile([P, CW * NT], F32, name="xT")
+        x_raw = keep.tile([P, T_TILES * DV], BF16, name="x_raw")
+        xT = [keep.tile([P, CW * BANK], F32, name="xT%d" % h) for h in range(HALVES)]
+        XT = [keep.tile([P, CW * P], F32, name="XT%d" % i) for i in range(I_TILES)]
         z_raw = keep.tile([P, GROUPS * 4 * DY], BF16, name="z_raw")
         z_grouped = keep.tile([P, GROUPS * DY * 4], BF16, name="z_grouped", align_bytes=64)
         z_codes = keep.tile([P, GROUPS * DY], U32, name="z_codes", align_bytes=64)
         z_scales = keep.tile([P, GROUPS * DY], U8, name="z_scales", align_bytes=64)
-        kin_codes = keep.tile([P, I_TILES * PASS], U32, name="kin_codes", align_bytes=64)
-        kin_scales = keep.tile([P, I_TILES * PASS], U8, name="kin_scales", align_bytes=64)
         k_codes = keep.tile([P, GROUPS * NT], U32, name="k_codes", align_bytes=64)
         k_scales = keep.tile([P, GROUPS * NT], U8, name="k_scales", align_bytes=64)
         lam_codes = keep.tile([P, GROUPS * DY], U32, name="lam_codes", align_bytes=64)
         lam_scales = keep.tile([P, GROUPS * DY], U8, name="lam_scales", align_bytes=64)
-        y_raw = keep.tile([P, NT // P * DY], BF16, name="y_raw")
-        h_raw = keep.tile([P, NT // P * DY], BF16, name="h_raw")
-        partial = keep.tile([P, NT // P * DY], F32, name="partial")
+        y_raw = keep.tile([P, T_TILES * DY], BF16, name="y_raw")
+        h_raw = keep.tile([P, T_TILES * DY], BF16, name="h_raw")
+        y_plus_h = keep.tile([P, T_TILES * DY], F32, name="y_plus_h")
 
-        xT_pairs = xT[:].bitcast(BF16).rearrange("p (w t e) -> p w t e", w=CW, e=2)
         X_raw = {}
-        XT = {}
         kin_raw = {}
         kin_grouped = {}
+        kin_codes = {}
+        kin_scales = {}
         k_rows = {}
         k_grouped = {}
         lam_rows = {}
         lam_grouped = {}
-        tr_bank = {}
+        now = {"unit": 0, "job": 0, "lam_unit": Z_UNIT}
+        transpose_jobs = []
+        vector_work = {}
+        tensor_work = {}
 
-        def load_X(g):
-            X_raw[g] = ring.tile([P, 4 * DV], BF16, name="X_raw", tag="X_raw", bufs=2)
+        def at(table, unit, job):
+            table.setdefault(unit, []).append(job)
+
+        def load_X(g, first, count):
+            if first == 0:
+                X_raw[g] = ring.tile([P, 4 * DV], BF16, name="X_raw", tag="X_raw", bufs=2)
             nc.sync.dma_start(
-                out=X_raw[g][:].rearrange("p (q c) -> p q c", q=4), in_=X_rows[g]
+                out=X_raw[g][:, first * DV : (first + count) * DV].rearrange(
+                    "p (q c) -> p q c", q=count
+                ),
+                in_=X_rows[g][:, first : first + count, :],
             )
 
         def load_kin(it):
@@ -102,14 +113,55 @@ def tile_condtransportkernel_pb_kernel(
                 identity=ident[:],
             )
 
-        def sum_of_squares(rows, q, result_column):
+        def transpose_rows(raw, q, turned):
+            bank = new_transpose_bank()
+            for cw in range(CW):
+                transpose_words(bank, cw, raw, q * ROW_WORDS + cw * P)
+            nc.vector.tensor_copy(
+                out=turned, in_=bank[:, 0 : CW * P].rearrange("p (w t) -> p w t", w=CW)
+            )
+
+        def half_sum_of_squares(rows, q, result_column):
             squares = ring.tile([P, DV], BF16, name="squares", tag="squares", bufs=2)
             nc.scalar.activation(
                 out=squares[:],
                 in_=rows[:, q * DV : (q + 1) * DV],
                 func=ACT.Square,
+                scale=0.5 ** 0.5,
                 accum_out=result_column,
             )
+
+        def transpose_X_tile(g, j):
+            transpose_rows(X_raw[g], j, XT[4 * g + j][:].rearrange("p (w t) -> p w t", w=CW))
+            half_sum_of_squares(X_raw[g], j, X_sq_half[:, 4 * g + j : 4 * g + j + 1])
+
+        def transpose_kin(it, part):
+            bank = new_transpose_bank()
+            for pos in range(4):
+                transpose_words(bank, pos, kin_raw[it], part * BANK + pos * P)
+            if part == 0:
+                kin_grouped[it] = ring.tile(
+                    [P, NX // 2], F32, name="kin_grouped", tag="kin_grouped", bufs=3,
+                    align_bytes=64,
+                )
+            nc.scalar.copy(
+                out=kin_grouped[it][:].rearrange("p (g i u) -> p g i u", g=GROUPS, u=2)[
+                    :, 2 * part : 2 * part + 2
+                ],
+                in_=bank[:].rearrange("p (b u i) -> p b i u", b=2, u=2),
+            )
+            if part == 1:
+                if it + KIN_BUFS < I_TILES:
+                    load_kin(it + KIN_BUFS)
+                at(vector_work, now["unit"] + QUANTISE_LAG, lambda: quantise_kin(it))
+                now["lam_unit"] = max(now["unit"] + LAM_LAG, now["lam_unit"] + 1)
+                at(tensor_work, now["lam_unit"], lambda: lam_tile(it))
+
+        def next_transpose_job():
+            if now["job"] < len(transpose_jobs):
+                job = transpose_jobs[now["job"]]
+                now["job"] += 1
+                job()
 
         def spread_query_norms(th):
             bank = new_transpose_bank()
@@ -117,133 +169,23 @@ def tile_condtransportkernel_pb_kernel(
                 tile_col = 4 * th + q
                 nc.tensor.matmul(
                     out=bank[:, q * P : (q + 1) * P],
-                    lhsT=x_sq[:, tile_col : tile_col + 1].to_broadcast([P, P]),
-                    rhs=half_ident[:],
+                    lhsT=x_sq_half[:, tile_col : tile_col + 1].to_broadcast([P, P]),
+                    rhs=ident[:],
                     start=True,
                     stop=True,
                 )
             nc.vector.tensor_copy(out=x_sq_half_all[:, th * BANK : (th + 1) * BANK], in_=bank[:])
 
-        make_identity(nc, ident[:])
-        nc.vector.memset(zero_col[:], 0.0)
-        nc.scalar.activation(out=one_col[:], in_=zero_col[:], func=ACT.Exp)
-        nc.vector.tensor_scalar_mul(out=half_ident[:], in0=ident[:], scalar1=0.5)
-
-        for h in range(HALVES):
-            nc.sync.dma_start(
-                out=x_raw[h][:].rearrange("p (q c) -> p q c", q=4), in_=x_rows[h]
-            )
-        load_X(0)
-        load_kin(0)
-        nc.sync.dma_start(out=z_raw[:].rearrange("p (a r) -> p a r", r=2 * DY), in_=Z_rows)
-        load_X(1)
-        for it in range(1, KIN_BUFS - 1):
-            load_kin(it)
-
-        for h in range(HALVES):
-            for cw in range(CW):
-                bank = new_transpose_bank()
-                for q in range(4):
-                    transpose_words(bank, q, x_raw[h], q * ROW_WORDS + cw * P)
-                nc.vector.tensor_copy(
-                    out=xT[:, cw * NT + h * BANK : cw * NT + (h + 1) * BANK], in_=bank[:]
-                )
-        XT[0] = ring.tile([P, CW * PASS], F32, name="XT", tag="XT", bufs=2)
-        for cw in range(CW):
-            bank = new_transpose_bank()
-            for q in range(4):
-                transpose_words(bank, q, X_raw[0], q * ROW_WORDS + cw * P)
-            nc.vector.tensor_copy(out=XT[0][:, cw * PASS : (cw + 1) * PASS], in_=bank[:])
-        for q in range(4):
-            sum_of_squares(x_raw[0], q, x_sq[:, q : q + 1])
-        for q in range(4):
-            sum_of_squares(X_raw[0], q, X_sq[:, q : q + 1])
-        nc.vector.tensor_scalar_mul(out=X_sq_half[:, 0:4], in0=X_sq[:, 0:4], scalar1=0.5)
-        for q in range(4):
-            sum_of_squares(x_raw[1], q, x_sq[:, 4 + q : 5 + q])
-
-        z_by_column = z_raw[:].rearrange("p (g t d) -> p g d t", g=GROUPS, t=4)
-        z_words = z_grouped[:].rearrange("p (g d t) -> p g d t", g=GROUPS, t=4)
-        for g in range(GROUPS):
-            nc.gpsimd.tensor_scalar(
-                out=z_words[:, g], in0=z_by_column[:, g], scalar1=1.0, scalar2=0.0,
-                op0=ALU.mult, op1=ALU.add,
-            )
-
-        def weave(r, m):
-            g_next = r // 4 + 1
-            jobs = [("kin", 0), ("kin", 1)]
-            if r % 4 >= 1 and g_next < GROUPS:
-                jobs = [("X", r % 4 - 1)] + jobs
-            b, pos = divmod(m, 4)
-            if b >= len(jobs):
-                return
-            kind, part = jobs[b]
-            if pos == 0:
-                tr_bank[b] = new_transpose_bank()
-            bank = tr_bank[b]
-            if kind == "X":
-                transpose_words(bank, pos, X_raw[g_next], pos * ROW_WORDS + part * P)
-                if pos == 3:
-                    if part == 0:
-                        XT[g_next] = ring.tile([P, CW * PASS], F32, name="XT", tag="XT", bufs=2)
-                    nc.vector.tensor_copy(
-                        out=XT[g_next][:, part * PASS : (part + 1) * PASS], in_=bank[:]
-                    )
-            else:
-                transpose_words(bank, pos, kin_raw[r], part * BANK + pos * P)
-                if pos == 3:
-                    if part == 0:
-                        kin_grouped[r] = ring.tile(
-                            [P, NX // 2], F32, name="kin_grouped", tag="kin_grouped", bufs=2,
-                            align_bytes=64,
-                        )
-                    nc.scalar.copy(
-                        out=kin_grouped[r][:].rearrange("p (g i u) -> p g i u", g=GROUPS, u=2)[
-                            :, 2 * part : 2 * part + 2
-                        ],
-                        in_=bank[:].rearrange("p (b u i) -> p b i u", b=2, u=2),
-                    )
-
-        def gram_unit(r, unit):
-            n = 2 * r + unit
-            g, th, j = n // 8, (n % 8) // 4, n % 4
-            X_pairs = XT[g][:].bitcast(BF16).rearrange("p (w i e) -> p w i e", w=CW, e=2)
-            gram = psum.tile([P, BANK], F32, name="gram", tag="gram", bufs=3)
-            for kc in range(UNIT_MATMULS):
-                cw, e = divmod(kc, 2)
-                nc.tensor.matmul(
-                    out=gram[:],
-                    lhsT=X_pairs[:, cw, j * P : (j + 1) * P, e],
-                    rhs=xT_pairs[:, cw, th * BANK : (th + 1) * BANK, e],
-                    start=(kc == 0),
-                    stop=(kc == UNIT_MATMULS - 1),
-                )
-                weave(r, unit * UNIT_MATMULS + kc)
-            if g == 0 and j == 0:
-                spread_query_norms(th)
-            minus_half_d2 = ring.tile([P, BANK], F32, name="minus_half_d2", tag="mhd2", bufs=3)
-            nc.vector.scalar_tensor_tensor(
-                out=minus_half_d2[:],
-                in0=gram[:],
-                scalar=X_sq_half[:, 4 * g + j : 4 * g + j + 1],
-                in1=x_sq_half_all[:, th * BANK : (th + 1) * BANK],
-                op0=ALU.subtract,
-                op1=ALU.subtract,
-            )
-            if j == 0:
-                k_rows[(g, th)] = ring.tile([P, 4 * BANK], BF16, name="k_rows", tag="k_rows", bufs=2)
-            nc.scalar.activation(
-                out=k_rows[(g, th)][:, j * BANK : (j + 1) * BANK],
-                in_=minus_half_d2[:],
-                func=ACT.Exp,
-                scale=1.0 / 64.0,
-            )
-
         def quantise_kin(it):
+            kin_codes[it] = ring.tile(
+                [P, PASS], U32, name="kin_codes", tag="kin_codes", bufs=6, align_bytes=64
+            )
+            kin_scales[it] = ring.tile(
+                [P, PASS], U8, name="kin_scales", tag="kin_scales", bufs=6, align_bytes=64
+            )
             nc.vector.quantize_mx(
-                out=kin_codes[:, it * PASS : (it + 1) * PASS].bitcast(FP8X4),
-                scales=kin_scales[:, it * PASS : (it + 1) * PASS],
+                out=kin_codes[it][:].bitcast(FP8X4),
+                scales=kin_scales[it][:],
                 in_=kin_grouped[it][:].bitcast(BF16),
             )
 
@@ -253,8 +195,8 @@ def tile_condtransportkernel_pb_kernel(
             for c in range(GROUPS):
                 nc.tensor.matmul_mx(
                     out=acc[:, 0:DY],
-                    lhsT=kin_codes[:, it * PASS + c * P : it * PASS + (c + 1) * P].bitcast(FP8X4),
-                    lhsT_scale=kin_scales[:, it * PASS + c * P : it * PASS + (c + 1) * P],
+                    lhsT=kin_codes[it][:, c * P : (c + 1) * P].bitcast(FP8X4),
+                    lhsT_scale=kin_scales[it][:, c * P : (c + 1) * P],
                     rhs=z_codes[:, c * DY : (c + 1) * DY].bitcast(FP8X4),
                     rhs_scale=z_scales[:, c * DY : (c + 1) * DY],
                     start=(c == 0),
@@ -263,33 +205,9 @@ def tile_condtransportkernel_pb_kernel(
             if j == 0:
                 lam_rows[g] = ring.tile([P, 4 * DY], BF16, name="lam_rows", tag="lam_rows", bufs=2)
             nc.scalar.copy(out=lam_rows[g][:, j * DY : (j + 1) * DY], in_=acc[:, 0:DY])
-
-        def k_block(r):
-            quad, side = r // 2 - 1, r % 2
-            g, th = divmod(quad, HALVES)
-            return g, th, side * (BANK // 2)
-
-        def regroup_k(r):
-            g, th, first = k_block(r)
-            k_grouped[r] = ring.tile(
-                [P, 2 * BANK], BF16, name="k_grouped", tag="k_grouped", bufs=2, align_bytes=64
-            )
-            nc.vector.tensor_scalar_min(
-                out=k_grouped[r][:].rearrange("p (w j) -> p w j", j=4),
-                in0=k_rows[(g, th)][:].rearrange("p (j w) -> p w j", j=4)[
-                    :, first : first + BANK // 2
-                ],
-                scalar1=1.0,
-            )
-
-        def quantise_k(r):
-            g, th, first = k_block(r)
-            col = g * NT + th * BANK + first
-            nc.vector.quantize_mx(
-                out=k_codes[:, col : col + BANK // 2].bitcast(FP8X4),
-                scales=k_scales[:, col : col + BANK // 2],
-                in_=k_grouped[r][:],
-            )
+            if j == 3:
+                at(vector_work, now["unit"] + 1, lambda: regroup_lam(g))
+                at(vector_work, now["unit"] + 2, lambda: quantise_lam(g))
 
         def regroup_lam(g):
             lam_grouped[g] = ring.tile(
@@ -307,80 +225,206 @@ def tile_condtransportkernel_pb_kernel(
                 in_=lam_grouped[g][:],
             )
 
-        def regression_passes(pair, groups):
-            acc = psum.tile([P, BANK], F32, name="mx", tag="mx", bufs=2)
-            for s in range(2):
-                t0 = (2 * pair + s) * P
-                for g in groups:
-                    nc.tensor.matmul_mx(
-                        out=acc[:, s * DY : (s + 1) * DY],
-                        lhsT=k_codes[:, g * NT + t0 : g * NT + t0 + P].bitcast(FP8X4),
-                        lhsT_scale=k_scales[:, g * NT + t0 : g * NT + t0 + P],
-                        rhs=lam_codes[:, g * DY : (g + 1) * DY].bitcast(FP8X4),
-                        rhs_scale=lam_scales[:, g * DY : (g + 1) * DY],
-                        start=(g == groups[0]),
-                        stop=(g == groups[-1]),
-                    )
-            return acc
+        def kernel_values(g, th, j, gram, first, count):
+            minus_half_d2 = ring.tile([P, BANK], F32, name="minus_half_d2", tag="mhd2", bufs=6)
+            nc.vector.scalar_tensor_tensor(
+                out=minus_half_d2[:, 0:count],
+                in0=gram[:, first : first + count],
+                scalar=X_sq_half[:, 4 * g + j : 4 * g + j + 1],
+                in1=x_sq_half_all[:, th * BANK + first : th * BANK + first + count],
+                op0=ALU.subtract,
+                op1=ALU.subtract,
+            )
+            nc.scalar.activation(
+                out=k_rows[(g, th)][:, j * BANK + first : j * BANK + first + count],
+                in_=minus_half_d2[:, 0:count],
+                func=ACT.Exp,
+                scale=1.0 / 64.0,
+            )
 
-        early_groups = list(range(GROUPS - 1))
-        for r in range(ROUNDS + LAM_LAG):
-            g_next = r // 4 + 1
-            if r + KIN_BUFS - 1 < I_TILES:
-                load_kin(r + KIN_BUFS - 1)
-            if r % 4 == 2 and g_next + 1 < GROUPS:
-                load_X(g_next + 1)
-            if r == 4:
-                nc.sync.dma_start(out=y_raw[:].rearrange("p (a d) -> p a d", d=DY), in_=y_rows)
-                nc.sync.dma_start(out=h_raw[:].rearrange("p (a d) -> p a d", d=DY), in_=h_rows)
-                nc.gpsimd.tensor_tensor(out=partial[:], in0=y_raw[:], in1=h_raw[:], op=ALU.add)
-            if r >= LAM_LAG:
-                lam_tile(r - LAM_LAG)
+        def regroup_k(g, th, piece):
+            k_grouped[(g, th, piece)] = ring.tile(
+                [P, 4 * PIECE], BF16, name="k_grouped", tag="k_grouped", bufs=2, align_bytes=64
+            )
+            nc.vector.tensor_scalar_min(
+                out=k_grouped[(g, th, piece)][:].rearrange("p (w j) -> p w j", j=4),
+                in0=k_rows[(g, th)][:].rearrange("p (j w) -> p w j", j=4)[
+                    :, piece * PIECE : (piece + 1) * PIECE
+                ],
+                scalar1=1.0,
+            )
 
-            if r < ROUNDS:
-                gram_unit(r, 0)
-            if r == 1:
-                nc.vector.quantize_mx(
-                    out=z_codes[:].bitcast(FP8X4), scales=z_scales[:], in_=z_grouped[:]
+        def quantise_k(g, th, piece):
+            col = g * NT + th * BANK + piece * PIECE
+            nc.vector.quantize_mx(
+                out=k_codes[:, col : col + PIECE].bitcast(FP8X4),
+                scales=k_scales[:, col : col + PIECE],
+                in_=k_grouped[(g, th, piece)][:],
+            )
+
+        def gram_unit(u):
+            g, th, j = u // 8, (u % 8) // 4, u % 4
+            now["unit"] = u
+            for job in tensor_work.get(u, []):
+                job()
+            for job in vector_work.get(u, []):
+                job()
+            X_pairs = XT[4 * g + j][:].bitcast(BF16).rearrange("p (w i e) -> p w i e", w=CW, e=2)
+            x_pairs = xT[th][:].bitcast(BF16).rearrange("p (w t e) -> p w t e", w=CW, e=2)
+            gram = psum.tile([P, BANK], F32, name="gram", tag="gram", bufs=3)
+            job_slots = (0, 2, 4) if u < 3 else (1, 4)
+            for kc in range(UNIT_MATMULS):
+                cw, e = divmod(kc, 2)
+                nc.tensor.matmul(
+                    out=gram[:],
+                    lhsT=X_pairs[:, cw, :, e],
+                    rhs=x_pairs[:, cw, :, e],
+                    start=(kc == 0),
+                    stop=(kc == UNIT_MATMULS - 1),
                 )
-            if 1 <= r <= ROUNDS:
-                quantise_kin(r - 1)
-            if r >= 2:
-                regroup_k(r)
-            if r < ROUNDS and g_next < GROUPS:
-                col = 4 * g_next + r % 4
-                sum_of_squares(X_raw[g_next], r % 4, X_sq[:, col : col + 1])
-            if ROUNDS - 2 <= r < ROUNDS:
-                for pair in (2 * (r - ROUNDS + 2), 2 * (r - ROUNDS + 2) + 1):
-                    acc = regression_passes(pair, early_groups)
-                    cols = slice(pair * BANK, (pair + 1) * BANK)
-                    nc.vector.tensor_tensor(
-                        out=partial[:, cols], in0=acc[:], in1=partial[:, cols], op=ALU.add
-                    )
+                if kc in job_slots:
+                    next_transpose_job()
+            if g == 0 and j == 0:
+                spread_query_norms(th)
+            if j == 0:
+                k_rows[(g, th)] = ring.tile([P, 4 * BANK], BF16, name="k_rows", tag="k_rows", bufs=2)
+            return gram
 
-            if r < ROUNDS:
-                gram_unit(r, 1)
-            lam_group_done = r >= LAM_LAG and (r - LAM_LAG) % 4 == 3
-            if lam_group_done:
-                regroup_lam((r - LAM_LAG) // 4)
-            if r >= 2:
-                quantise_k(r)
-            if lam_group_done:
-                quantise_lam((r - LAM_LAG) // 4)
-            if r % 4 == 3 and g_next < GROUPS:
-                nc.vector.tensor_scalar_mul(
-                    out=X_sq_half[:, 4 * g_next : 4 * g_next + 4],
-                    in0=X_sq[:, 4 * g_next : 4 * g_next + 4],
-                    scalar1=0.5,
+        def regression_passes(acc, t_tile, groups, first, last):
+            t0 = t_tile * P
+            for g in groups:
+                nc.tensor.matmul_mx(
+                    out=acc,
+                    lhsT=k_codes[:, g * NT + t0 : g * NT + t0 + P].bitcast(FP8X4),
+                    lhsT_scale=k_scales[:, g * NT + t0 : g * NT + t0 + P],
+                    rhs=lam_codes[:, g * DY : (g + 1) * DY].bitcast(FP8X4),
+                    rhs_scale=lam_scales[:, g * DY : (g + 1) * DY],
+                    start=(first and g == groups[0]),
+                    stop=(last and g == groups[-1]),
                 )
 
-        for pair in range(NT // P // 2):
-            acc = regression_passes(pair, [GROUPS - 1])
-            result = ring.tile([P, BANK], F32, name="result", tag="result", bufs=2)
+        def finish(acc, first_tile, count):
+            result = ring.tile([P, BANK], F32, name="result", tag="result", bufs=6)
             nc.vector.tensor_tensor(
-                out=result[:], in0=acc[:], in1=partial[:, pair * BANK : (pair + 1) * BANK], op=ALU.add
+                out=result[:, 0 : count * DY],
+                in0=acc,
+                in1=y_plus_h[:, first_tile * DY : (first_tile + count) * DY],
+                op=ALU.add,
             )
             nc.sync.dma_start(
-                out=out_rows[:, 2 * pair : 2 * pair + 2, :],
-                in_=result[:].rearrange("p (a d) -> p a d", d=DY),
+                out=out_rows[:, first_tile : first_tile + count, :],
+                in_=result[:, 0 : count * DY].rearrange("p (a d) -> p a d", d=DY),
             )
+
+        make_identity(nc, ident[:])
+        nc.vector.memset(zero_col[:], 0.0)
+        nc.scalar.activation(out=one_col[:], in_=zero_col[:], func=ACT.Exp)
+
+        for q in range(4):
+            nc.sync.dma_start(out=x_raw[:, q * DV : (q + 1) * DV], in_=x_tiles[q])
+        load_X(0, 0, 1)
+        load_X(0, 1, 3)
+        nc.sync.dma_start(
+            out=x_raw[:, 4 * DV : 8 * DV].rearrange("p (q c) -> p q c", q=4), in_=x_halves[1]
+        )
+        load_kin(0)
+        load_X(1, 0, 4)
+        load_kin(1)
+        nc.sync.dma_start(out=z_raw[:].rearrange("p (a r) -> p a r", r=2 * DY), in_=Z_rows)
+        for it in range(2, KIN_BUFS):
+            load_kin(it)
+
+        def transpose_x_tile(q):
+            h, q4 = divmod(q, 4)
+            transpose_rows(
+                x_raw, q,
+                xT[h][:].rearrange("p (w t) -> p w t", w=CW)[:, :, q4 * P : (q4 + 1) * P],
+            )
+            half_sum_of_squares(x_raw, q, x_sq_half[:, q : q + 1])
+
+        for q in range(4):
+            transpose_x_tile(q)
+        transpose_X_tile(0, 0)
+
+        for j in range(1, 4):
+            transpose_jobs.append(lambda j=j: transpose_X_tile(0, j))
+
+        for q in range(4, T_TILES):
+            transpose_jobs.append(lambda q=q: transpose_x_tile(q))
+        kin_halves = [(it, part) for it in range(I_TILES) for part in range(2)]
+        taken = 0
+        for g in range(1, GROUPS):
+            for j in range(4):
+                between = 3 if g > 1 else 2 if j == 0 else 1
+                for it, part in kin_halves[taken : taken + between]:
+                    transpose_jobs.append(lambda it=it, part=part: transpose_kin(it, part))
+                taken += between
+                transpose_jobs.append(lambda g=g, j=j: transpose_X_tile(g, j))
+        for it, part in kin_halves[taken:]:
+            transpose_jobs.append(lambda it=it, part=part: transpose_kin(it, part))
+
+        z_by_column = z_raw[:].rearrange("p (g t d) -> p g d t", g=GROUPS, t=4)
+        z_words = z_grouped[:].rearrange("p (g d t) -> p g d t", g=GROUPS, t=4)
+        for g in range(GROUPS):
+            nc.gpsimd.tensor_scalar(
+                out=z_words[:, g], in0=z_by_column[:, g], scalar1=1.0, scalar2=0.0,
+                op0=ALU.mult, op1=ALU.add,
+            )
+        at(
+            vector_work, Z_UNIT,
+            lambda: nc.vector.quantize_mx(
+                out=z_codes[:].bitcast(FP8X4), scales=z_scales[:], in_=z_grouped[:]
+            ),
+        )
+
+        for u in range(UNITS):
+            g, th, j = u // 8, (u % 8) // 4, u % 4
+            if u % 8 == 2 and g + 2 < GROUPS:
+                load_X(g + 2, 0, 4)
+            if u == 8:
+                nc.sync.dma_start(out=y_raw[:].rearrange("p (a d) -> p a d", d=DY), in_=y_rows)
+                nc.sync.dma_start(out=h_raw[:].rearrange("p (a d) -> p a d", d=DY), in_=h_rows)
+                for pair in range(T_TILES // 2):
+                    cols = slice(pair * BANK, (pair + 1) * BANK)
+                    nc.gpsimd.tensor_tensor(
+                        out=y_plus_h[:, cols], in0=y_raw[:, cols], in1=h_raw[:, cols], op=ALU.add
+                    )
+            gram = gram_unit(u)
+            if u < UNITS - 1:
+                kernel_values(g, th, j, gram, 0, BANK)
+                if j == 3:
+                    at(vector_work, u + 2, lambda g=g, th=th: regroup_k(g, th, 0))
+                    at(vector_work, u + 3, lambda g=g, th=th: quantise_k(g, th, 0))
+                    at(vector_work, u + 3, lambda g=g, th=th: regroup_k(g, th, 1))
+                    at(vector_work, u + 4, lambda g=g, th=th: quantise_k(g, th, 1))
+
+        assert max(vector_work) < UNITS and max(tensor_work) < UNITS and now["job"] == len(transpose_jobs)
+
+        last_g, last_th = GROUPS - 1, HALVES - 1
+        for piece in range(2):
+            kernel_values(last_g, last_th, 3, gram, piece * PIECE, PIECE)
+        early_groups = list(range(GROUPS - 1))
+        all_groups = list(range(GROUPS))
+        waiting = {}
+        for t_tile in range(4, T_TILES):
+            waiting[t_tile] = (
+                new_transpose_bank()
+                if t_tile < T_TILES - 1
+                else psum.tile([P, BANK], F32, name="mx", tag="mx", bufs=2)
+            )
+            regression_passes(waiting[t_tile][:, 0:DY], t_tile, early_groups, True, False)
+        for piece in range(2):
+            regroup_k(last_g, last_th, piece)
+        for piece in range(2):
+            quantise_k(last_g, last_th, piece)
+        acc = psum.tile([P, BANK], F32, name="mx", tag="mx", bufs=2)
+        for s in range(2):
+            regression_passes(acc[:, s * DY : (s + 1) * DY], s, all_groups, True, True)
+        finish(acc[:], 0, 2)
+        for t_tile in range(4, T_TILES):
+            regression_passes(waiting[t_tile][:, 0:DY], t_tile, [last_g], False, True)
+            finish(waiting[t_tile][:, 0:DY], t_tile, 1)
+        acc = psum.tile([P, BANK], F32, name="gram", tag="gram", bufs=3)
+        for s in range(2):
+            regression_passes(acc[:, s * DY : (s + 1) * DY], 2 + s, all_groups, True, True)
+        finish(acc[:], 2, 2)

@@ -167,12 +167,10 @@ def tile_condtransportkernel_pb_kernel(
             bank = new_transpose_bank()
             for q in range(4):
                 tile_col = 4 * th + q
-                nc.tensor.matmul(
+                nc.tensor.transpose(
                     out=bank[:, q * P : (q + 1) * P],
-                    lhsT=x_sq_half[:, tile_col : tile_col + 1].to_broadcast([P, P]),
-                    rhs=ident[:],
-                    start=True,
-                    stop=True,
+                    in_=x_sq_half[:, tile_col : tile_col + 1].to_broadcast([P, P]),
+                    identity=ident[:],
                 )
             nc.vector.tensor_copy(out=x_sq_half_all[:, th * BANK : (th + 1) * BANK], in_=bank[:])
 

@@ -52,6 +52,7 @@ def tile_condtransportkernel_pb_kernel(
         ctx.enter_context(tc.manual_schedule())
 
         ident = keep.tile([P, P], F32, name="ident")
+        zeros = keep.tile([P, BANK], BF16, name="zeros")
         zero_col = keep.tile([P, 1], F32, name="zero_col")
         one_col = keep.tile([P, 1], F32, name="one_col")
         x_sq_half = keep.tile([P, T_TILES], F32, name="x_sq_half")
@@ -314,6 +315,7 @@ def tile_condtransportkernel_pb_kernel(
                 in_=result[:, 0 : count * DY].rearrange("p (a d) -> p a d", d=DY),
             )
 
+        nc.vector.memset(zeros[:], 0.0)
         make_identity(nc, ident[:])
         nc.vector.memset(zero_col[:], 0.0)
         nc.scalar.activation(out=one_col[:], in_=zero_col[:], func=ACT.Exp)
@@ -332,6 +334,17 @@ def tile_condtransportkernel_pb_kernel(
         for it in range(2, KIN_BUFS):
             load_kin(it)
 
+        idle_bank = psum.tile([P, BANK], F32, name="mx", tag="mx", bufs=2)
+
+        def idle_matmuls(count, width):
+            for n in range(count):
+                nc.tensor.matmul(
+                    out=idle_bank[:, 0:width], lhsT=zeros[:, 0:P], rhs=zeros[:, 0:width],
+                    start=True, stop=True,
+                )
+
+        idle_matmuls(4, BANK)
+
         def transpose_x_tile(q):
             h, q4 = divmod(q, 4)
             transpose_rows(
@@ -342,7 +355,9 @@ def tile_condtransportkernel_pb_kernel(
 
         for q in range(4):
             transpose_x_tile(q)
+            idle_matmuls(1, BANK // 2)
         transpose_X_tile(0, 0)
+        idle_matmuls(1, BANK)
 
         for j in range(1, 4):
             transpose_jobs.append(lambda j=j: transpose_X_tile(0, j))

@@ -25,8 +25,8 @@ UNIT_MATMULS = 2 * CW
 UNITS = I_TILES * HALVES
 PIECE = BANK // 2
 KIN_BUFS = 6
-QUANTISE_LAG = 1
-LAM_LAG = 3
+QUANTISE_LAG = 2
+LAM_LAG = 4
 Z_UNIT = 8
 
 FLOPS = 2 * NX * NX * DY + 2 * NX * NT * DV + 2 * NT * NX * DY
@@ -228,7 +228,7 @@ def tile_condtransportkernel_pb_kernel(
             minus_half_d2 = ring.tile([P, BANK], F32, name="minus_half_d2", tag="mhd2", bufs=6)
             nc.vector.scalar_tensor_tensor(
                 out=minus_half_d2[:, 0:count],
-                in0=gram[:, first : first + count],
+                in0=gram[:, 0:count],
                 scalar=X_sq_half[:, 4 * g + j : 4 * g + j + 1],
                 in1=x_sq_half_all[:, th * BANK + first : th * BANK + first + count],
                 op0=ALU.subtract,
@@ -261,8 +261,7 @@ def tile_condtransportkernel_pb_kernel(
                 in_=k_grouped[(g, th, piece)][:],
             )
 
-        def gram_unit(u):
-            g, th, j = u // 8, (u % 8) // 4, u % 4
+        def gram_unit(u, g, th, j, first, count):
             now["unit"] = u
             for job in tensor_work.get(u, []):
                 job()
@@ -271,13 +270,13 @@ def tile_condtransportkernel_pb_kernel(
             X_pairs = XT[4 * g + j][:].bitcast(BF16).rearrange("p (w i e) -> p w i e", w=CW, e=2)
             x_pairs = xT[th][:].bitcast(BF16).rearrange("p (w t e) -> p w t e", w=CW, e=2)
             gram = psum.tile([P, BANK], F32, name="gram", tag="gram", bufs=3)
-            job_slots = (0, 2, 4) if u < 3 else (1, 4)
+            job_slots = (1, 3, 5) if u < 3 else (1, 4)
             for kc in range(UNIT_MATMULS):
                 cw, e = divmod(kc, 2)
                 nc.tensor.matmul(
-                    out=gram[:],
+                    out=gram[:, 0:count],
                     lhsT=X_pairs[:, cw, :, e],
-                    rhs=x_pairs[:, cw, :, e],
+                    rhs=x_pairs[:, cw, first : first + count, e],
                     start=(kc == 0),
                     stop=(kc == UNIT_MATMULS - 1),
                 )
@@ -285,9 +284,9 @@ def tile_condtransportkernel_pb_kernel(
                     next_transpose_job()
             if g == 0 and j == 0:
                 spread_query_norms(th)
-            if j == 0:
+            if j == 0 and first == 0:
                 k_rows[(g, th)] = ring.tile([P, 4 * BANK], BF16, name="k_rows", tag="k_rows", bufs=2)
-            return gram
+            kernel_values(g, th, j, gram, first, count)
 
         def regression_passes(acc, t_tile, groups, first, last):
             t0 = t_tile * P
@@ -322,8 +321,8 @@ def tile_condtransportkernel_pb_kernel(
 
         for q in range(4):
             nc.sync.dma_start(out=x_raw[:, q * DV : (q + 1) * DV], in_=x_tiles[q])
-        load_X(0, 0, 1)
-        load_X(0, 1, 3)
+        for j in range(4):
+            load_X(0, j, 1)
         nc.sync.dma_start(
             out=x_raw[:, 4 * DV : 8 * DV].rearrange("p (q c) -> p q c", q=4), in_=x_halves[1]
         )
@@ -364,6 +363,8 @@ def tile_condtransportkernel_pb_kernel(
 
         for q in range(4, T_TILES):
             transpose_jobs.append(lambda q=q: transpose_x_tile(q))
+        for n in range(4):
+            transpose_jobs.append(lambda: None)
         kin_halves = [(it, part) for it in range(I_TILES) for part in range(2)]
         taken = 0
         for g in range(1, GROUPS):
@@ -390,8 +391,15 @@ def tile_condtransportkernel_pb_kernel(
             ),
         )
 
-        for u in range(UNITS):
-            g, th, j = u // 8, (u % 8) // 4, u % 4
+        last_g, last_th = GROUPS - 1, HALVES - 1
+        units = []
+        for g in range(GROUPS):
+            for th in range(HALVES):
+                widths = [PIECE, PIECE] if (g, th) == (last_g, last_th) else [BANK]
+                for n, count in enumerate(widths):
+                    for j in range(4):
+                        units.append((g, th, j, n * count, count))
+        for u, (g, th, j, first, count) in enumerate(units):
             if u % 8 == 2 and g + 2 < GROUPS:
                 load_X(g + 2, 0, 4)
             if u == 8:
@@ -402,42 +410,33 @@ def tile_condtransportkernel_pb_kernel(
                     nc.gpsimd.tensor_tensor(
                         out=y_plus_h[:, cols], in0=y_raw[:, cols], in1=h_raw[:, cols], op=ALU.add
                     )
-            gram = gram_unit(u)
-            if u < UNITS - 1:
-                kernel_values(g, th, j, gram, 0, BANK)
-                if j == 3:
-                    at(vector_work, u + 2, lambda g=g, th=th: regroup_k(g, th, 0))
-                    at(vector_work, u + 3, lambda g=g, th=th: quantise_k(g, th, 0))
-                    at(vector_work, u + 3, lambda g=g, th=th: regroup_k(g, th, 1))
-                    at(vector_work, u + 4, lambda g=g, th=th: quantise_k(g, th, 1))
+            gram_unit(u, g, th, j, first, count)
+            if j == 3 and count == BANK:
+                step = 2 if (g, th) == (last_g, last_th - 1) else 1
+                at(vector_work, u + 1 + step, lambda g=g, th=th: regroup_k(g, th, 0))
+                at(vector_work, u + 1 + 2 * step, lambda g=g, th=th: quantise_k(g, th, 0))
+                at(vector_work, u + 1 + 2 * step, lambda g=g, th=th: regroup_k(g, th, 1))
+                at(vector_work, u + 1 + 3 * step, lambda g=g, th=th: quantise_k(g, th, 1))
+            if j == 3 and count == PIECE and first == 0:
+                at(vector_work, u + 2, lambda: regroup_k(last_g, last_th, 0))
+                at(vector_work, u + 4, lambda: quantise_k(last_g, last_th, 0))
 
-        assert max(vector_work) < UNITS and max(tensor_work) < UNITS and now["job"] == len(transpose_jobs)
+        assert max(vector_work) < len(units) and max(tensor_work) < len(units)
+        assert now["job"] == len(transpose_jobs)
 
-        last_g, last_th = GROUPS - 1, HALVES - 1
-        for piece in range(2):
-            kernel_values(last_g, last_th, 3, gram, piece * PIECE, PIECE)
-        early_groups = list(range(GROUPS - 1))
+        regroup_k(last_g, last_th, 1)
+        quantise_k(last_g, last_th, 1)
         all_groups = list(range(GROUPS))
-        waiting = {}
-        for t_tile in range(4, T_TILES):
-            waiting[t_tile] = (
-                new_transpose_bank()
-                if t_tile < T_TILES - 1
-                else psum.tile([P, BANK], F32, name="mx", tag="mx", bufs=2)
+        for pair in range(T_TILES // 2 - 1):
+            acc = (
+                psum.tile([P, BANK], F32, name="mx", tag="mx", bufs=2)
+                if pair % 2 == 0
+                else new_transpose_bank()
             )
-            regression_passes(waiting[t_tile][:, 0:DY], t_tile, early_groups, True, False)
-        for piece in range(2):
-            regroup_k(last_g, last_th, piece)
-        for piece in range(2):
-            quantise_k(last_g, last_th, piece)
-        acc = psum.tile([P, BANK], F32, name="mx", tag="mx", bufs=2)
-        for s in range(2):
-            regression_passes(acc[:, s * DY : (s + 1) * DY], s, all_groups, True, True)
-        finish(acc[:], 0, 2)
-        for t_tile in range(4, T_TILES):
-            regression_passes(waiting[t_tile][:, 0:DY], t_tile, [last_g], False, True)
-            finish(waiting[t_tile][:, 0:DY], t_tile, 1)
-        acc = psum.tile([P, BANK], F32, name="gram", tag="gram", bufs=3)
-        for s in range(2):
-            regression_passes(acc[:, s * DY : (s + 1) * DY], 2 + s, all_groups, True, True)
-        finish(acc[:], 2, 2)
+            for s in range(2):
+                regression_passes(acc[:, s * DY : (s + 1) * DY], 2 * pair + s, all_groups, True, True)
+            finish(acc[:], 2 * pair, 2)
+        for t_tile in range(T_TILES - 2, T_TILES):
+            acc = new_transpose_bank()
+            regression_passes(acc[:, 0:DY], t_tile, all_groups, True, True)
+            finish(acc[:, 0:DY], t_tile, 1)

@@ -27,6 +27,9 @@ PIECE = BANK // 2
 KIN_BUFS = 6
 QUANTISE_LAG = 2
 LAM_LAG = 4
+X_LEAD = 3
+KIN_FIRST_UNIT = 6
+Y_UNIT = 22
 Z_UNIT = 8
 
 FLOPS = 2 * NX * NX * DY + 2 * NX * NT * DV + 2 * NT * NX * DY
@@ -261,6 +264,11 @@ def tile_condtransportkernel_pb_kernel(
                 in_=k_grouped[(g, th, piece)][:],
             )
 
+        def job_slots_of(u):
+            if u < 3:
+                return (1, 3, 5)
+            return (1, 4)
+
         def gram_unit(u, g, th, j, first, count):
             now["unit"] = u
             for job in tensor_work.get(u, []):
@@ -270,7 +278,7 @@ def tile_condtransportkernel_pb_kernel(
             X_pairs = XT[4 * g + j][:].bitcast(BF16).rearrange("p (w i e) -> p w i e", w=CW, e=2)
             x_pairs = xT[th][:].bitcast(BF16).rearrange("p (w t e) -> p w t e", w=CW, e=2)
             gram = psum.tile([P, BANK], F32, name="gram", tag="gram", bufs=3)
-            job_slots = (1, 3, 5) if u < 3 else (1, 4)
+            job_slots = job_slots_of(u)
             for kc in range(UNIT_MATMULS):
                 cw, e = divmod(kc, 2)
                 nc.tensor.matmul(
@@ -326,11 +334,9 @@ def tile_condtransportkernel_pb_kernel(
         nc.sync.dma_start(
             out=x_raw[:, 4 * DV : 8 * DV].rearrange("p (q c) -> p q c", q=4), in_=x_halves[1]
         )
-        load_kin(0)
-        load_X(1, 0, 4)
-        load_kin(1)
         nc.sync.dma_start(out=z_raw[:].rearrange("p (a r) -> p a r", r=2 * DY), in_=Z_rows)
-        for it in range(2, KIN_BUFS):
+        load_X(1, 0, 4)
+        for it in range(KIN_BUFS):
             load_kin(it)
 
         idle_bank = psum.tile([P, BANK], F32, name="mx", tag="mx", bufs=2)
@@ -363,19 +369,22 @@ def tile_condtransportkernel_pb_kernel(
 
         for q in range(4, T_TILES):
             transpose_jobs.append(lambda q=q: transpose_x_tile(q))
-        for n in range(4):
-            transpose_jobs.append(lambda: None)
         kin_halves = [(it, part) for it in range(I_TILES) for part in range(2)]
         taken = 0
-        for g in range(1, GROUPS):
-            for j in range(4):
-                between = 3 if g > 1 else 2 if j == 0 else 1
-                for it, part in kin_halves[taken : taken + between]:
-                    transpose_jobs.append(lambda it=it, part=part: transpose_kin(it, part))
-                taken += between
+        for u in range(3, UNITS):
+            g, j = (u + X_LEAD) // 8, (u + X_LEAD) % 8
+            places = len(job_slots_of(u))
+            if g < GROUPS and j < 4:
                 transpose_jobs.append(lambda g=g, j=j: transpose_X_tile(g, j))
-        for it, part in kin_halves[taken:]:
-            transpose_jobs.append(lambda it=it, part=part: transpose_kin(it, part))
+                places -= 1
+            for n in range(places):
+                if u >= KIN_FIRST_UNIT and taken < len(kin_halves):
+                    it, part = kin_halves[taken]
+                    transpose_jobs.append(lambda it=it, part=part: transpose_kin(it, part))
+                    taken += 1
+                else:
+                    transpose_jobs.append(lambda: None)
+        assert taken == len(kin_halves)
 
         z_by_column = z_raw[:].rearrange("p (g t d) -> p g d t", g=GROUPS, t=4)
         z_words = z_grouped[:].rearrange("p (g d t) -> p g d t", g=GROUPS, t=4)
@@ -402,7 +411,7 @@ def tile_condtransportkernel_pb_kernel(
         for u, (g, th, j, first, count) in enumerate(units):
             if u % 8 == 2 and g + 2 < GROUPS:
                 load_X(g + 2, 0, 4)
-            if u == 8:
+            if u == Y_UNIT:
                 nc.sync.dma_start(out=y_raw[:].rearrange("p (a d) -> p a d", d=DY), in_=y_rows)
                 nc.sync.dma_start(out=h_raw[:].rearrange("p (a d) -> p a d", d=DY), in_=h_rows)
                 for pair in range(T_TILES // 2):
@@ -422,7 +431,7 @@ def tile_condtransportkernel_pb_kernel(
                 at(vector_work, u + 4, lambda: quantise_k(last_g, last_th, 0))
 
         assert max(vector_work) < len(units) and max(tensor_work) < len(units)
-        assert now["job"] == len(transpose_jobs)
+        assert now["job"] >= len(transpose_jobs) - 2 * (len(units) - UNITS)
 
         regroup_k(last_g, last_th, 1)
         quantise_k(last_g, last_th, 1)

@@ -29,7 +29,6 @@ QUANTISE_LAG = 2
 LAM_LAG = 4
 X_LEAD = 3
 KIN_FIRST_UNIT = 6
-Y_UNIT = 22
 Z_UNIT = 8
 
 FLOPS = 2 * NX * NX * DY + 2 * NX * NT * DV + 2 * NT * NX * DY
@@ -336,7 +335,11 @@ def tile_condtransportkernel_pb_kernel(
         )
         nc.sync.dma_start(out=z_raw[:].rearrange("p (a r) -> p a r", r=2 * DY), in_=Z_rows)
         load_X(1, 0, 4)
-        for it in range(KIN_BUFS):
+        for it in range(2):
+            load_kin(it)
+        nc.sync.dma_start(out=y_raw[:].rearrange("p (a d) -> p a d", d=DY), in_=y_rows)
+        nc.sync.dma_start(out=h_raw[:].rearrange("p (a d) -> p a d", d=DY), in_=h_rows)
+        for it in range(2, KIN_BUFS):
             load_kin(it)
 
         idle_bank = psum.tile([P, BANK], F32, name="mx", tag="mx", bufs=2)
@@ -393,6 +396,11 @@ def tile_condtransportkernel_pb_kernel(
                 out=z_words[:, g], in0=z_by_column[:, g], scalar1=1.0, scalar2=0.0,
                 op0=ALU.mult, op1=ALU.add,
             )
+        for pair in range(T_TILES // 2):
+            cols = slice(pair * BANK, (pair + 1) * BANK)
+            nc.gpsimd.tensor_tensor(
+                out=y_plus_h[:, cols], in0=y_raw[:, cols], in1=h_raw[:, cols], op=ALU.add
+            )
         at(
             vector_work, Z_UNIT,
             lambda: nc.vector.quantize_mx(
@@ -411,21 +419,14 @@ def tile_condtransportkernel_pb_kernel(
         for u, (g, th, j, first, count) in enumerate(units):
             if u % 8 == 2 and g + 2 < GROUPS:
                 load_X(g + 2, 0, 4)
-            if u == Y_UNIT:
-                nc.sync.dma_start(out=y_raw[:].rearrange("p (a d) -> p a d", d=DY), in_=y_rows)
-                nc.sync.dma_start(out=h_raw[:].rearrange("p (a d) -> p a d", d=DY), in_=h_rows)
-                for pair in range(T_TILES // 2):
-                    cols = slice(pair * BANK, (pair + 1) * BANK)
-                    nc.gpsimd.tensor_tensor(
-                        out=y_plus_h[:, cols], in0=y_raw[:, cols], in1=h_raw[:, cols], op=ALU.add
-                    )
             gram_unit(u, g, th, j, first, count)
             if j == 3 and count == BANK:
                 step = 2 if (g, th) == (last_g, last_th - 1) else 1
-                at(vector_work, u + 1 + step, lambda g=g, th=th: regroup_k(g, th, 0))
-                at(vector_work, u + 1 + 2 * step, lambda g=g, th=th: quantise_k(g, th, 0))
-                at(vector_work, u + 1 + 2 * step, lambda g=g, th=th: regroup_k(g, th, 1))
-                at(vector_work, u + 1 + 3 * step, lambda g=g, th=th: quantise_k(g, th, 1))
+                start = u + 1 if step == 2 else u + 2
+                at(vector_work, start + step, lambda g=g, th=th: regroup_k(g, th, 0))
+                at(vector_work, start + 2 * step, lambda g=g, th=th: quantise_k(g, th, 0))
+                at(vector_work, start + 2 * step, lambda g=g, th=th: regroup_k(g, th, 1))
+                at(vector_work, start + 3 * step, lambda g=g, th=th: quantise_k(g, th, 1))
             if j == 3 and count == PIECE and first == 0:
                 at(vector_work, u + 2, lambda: regroup_k(last_g, last_th, 0))
                 at(vector_work, u + 4, lambda: quantise_k(last_g, last_th, 0))

from contextlib import ExitStack

import concourse.mybir as mybir
from concourse.masks import make_identity

F32 = mybir.dt.float32
BF16 = mybir.dt.bfloat16
U32 = mybir.dt.uint32
U8 = mybir.dt.uint8
FP8X4 = mybir.dt.float8_e4m3fn_x4
ALU = mybir.AluOpType
ACT = mybir.ActivationFunctionType

P = 128
NX, NT, DV, DY = 2048, 1024, 768, 256
BANK = 512
PASS = 4 * P
GROUPS = NX // PASS
I_TILES = NX // P
T_TILES = NT // P
HALVES = NT // BANK
ROW_WORDS = DV // 2
CW = ROW_WORDS // P
UNIT_MATMULS = 2 * CW
UNITS = I_TILES * HALVES
PIECE = BANK // 2
KIN_BUFS = 6
QUANTISE_LAG = 2
LAM_LAG = 4
X_LEAD = 3
KIN_FIRST_UNIT = 6
Z_UNIT = 8

FLOPS = 2 * NX * NX * DY + 2 * NX * NT * DV + 2 * NT * NX * DY


def tile_condtransportkernel_pb_kernel(
    tc, x_var, X_var, Z_var, kXXvar_inv, y_var, h_mean, out
):
    nc = tc.nc
    x_tiles = x_var.rearrange("(a p) c -> a p c", p=P)
    x_halves = x_var.rearrange("(h q p) c -> h p q c", h=HALVES, p=P)
    X_rows = X_var.rearrange("(g q p) c -> g p q c", g=GROUPS, p=P)
    kin_rows = kXXvar_inv.rearrange("(i p) j -> i p j", p=P)
    Z_rows = Z_var.rearrange("(a q e) d -> q a (e d)", q=P, e=2)
    y_rows = y_var.rearrange("(a p) d -> p a d", p=P)
    h_rows = h_mean.rearrange("(a p) d -> p a d", p=P)
    out_rows = out.rearrange("(a p) d -> p a d", p=P)

    with ExitStack() as ctx:
        keep = ctx.enter_context(tc.tile_pool(name="keep", bufs=1))
        ring = ctx.enter_context(tc.tile_pool(name="ring", bufs=2))
        psum = ctx.enter_context(tc.psum_pool(name="psum", bufs=2))
        ctx.enter_context(tc.manual_schedule())

        ident = keep.tile([P, P], F32, name="ident")
        zeros = keep.tile([P, BANK], BF16, name="zeros")
        zero_col = keep.tile([P, 1], F32, name="zero_col")
        one_col = keep.tile([P, 1], F32, name="one_col")
        x_sq_half = keep.tile([P, T_TILES], F32, name="x_sq_half")
        X_sq_half = keep.tile([P, I_TILES], F32, name="X_sq_half")
        x_sq_half_all = keep.tile([P, NT], F32, name="x_sq_half_all")
        x_raw = keep.tile([P, T_TILES * DV], BF16, name="x_raw")
        xT = [keep.tile([P, CW * BANK], F32, name="xT%d" % h) for h in range(HALVES)]
        XT = [keep.tile([P, CW * P], F32, name="XT%d" % i) for i in range(I_TILES)]
        z_raw = keep.tile([P, GROUPS * 4 * DY], BF16, name="z_raw")
        z_grouped = keep.tile([P, GROUPS * DY * 4], BF16, name="z_grouped", align_bytes=64)
        z_codes = keep.tile([P, GROUPS * DY], U32, name="z_codes", align_bytes=64)
        z_scales = keep.tile([P, GROUPS * DY], U8, name="z_scales", align_bytes=64)
        k_codes = keep.tile([P, GROUPS * NT], U32, name="k_codes", align_bytes=64)
        k_scales = keep.tile([P, GROUPS * NT], U8, name="k_scales", align_bytes=64)
        lam_codes = keep.tile([P, GROUPS * DY], U32, name="lam_codes", align_bytes=64)
        lam_scales = keep.tile([P, GROUPS * DY], U8, name="lam_scales", align_bytes=64)
        y_raw = keep.tile([P, T_TILES * DY], BF16, name="y_raw")
        h_raw = keep.tile([P, T_TILES * DY], BF16, name="h_raw")
        y_plus_h = keep.tile([P, T_TILES * DY], F32, name="y_plus_h")

        X_raw = {}
        kin_raw = {}
        kin_grouped = {}
        kin_codes = {}
        kin_scales = {}
        k_rows = {}
        k_grouped = {}
        lam_rows = {}
        lam_grouped = {}
        now = {"unit": 0, "job": 0, "lam_unit": Z_UNIT}
        transpose_jobs = []
        vector_work = {}
        tensor_work = {}

        def at(table, unit, job):
            table.setdefault(unit, []).append(job)

        def load_X(g, first, count):
            if first == 0:
                X_raw[g] = ring.tile([P, 4 * DV], BF16, name="X_raw", tag="X_raw", bufs=2)
            nc.sync.dma_start(
                out=X_raw[g][:, first * DV : (first + count) * DV].rearrange(
                    "p (q c) -> p q c", q=count
                ),
                in_=X_rows[g][:, first : first + count, :],
            )

        def load_kin(it):
            kin_raw[it] = ring.tile([P, NX], BF16, name="kin_raw", tag="kin_raw", bufs=KIN_BUFS)
            nc.sync.dma_start(out=kin_raw[it][:], in_=kin_rows[it])

        def new_transpose_bank():
            return psum.tile([P, BANK], F32, name="tr", tag="tr", bufs=3)

        def transpose_words(bank, pos, raw, first_word):
            nc.tensor.transpose(
                out=bank[:, pos * P : (pos + 1) * P],
                in_=raw[:].bitcast(F32)[:, first_word : first_word + P],
                identity=ident[:],
            )

        def transpose_rows(raw, q, turned):
            bank = new_transpose_bank()
            for cw in range(CW):
                transpose_words(bank, cw, raw, q * ROW_WORDS + cw * P)
            nc.vector.tensor_copy(
                out=turned, in_=bank[:, 0 : CW * P].rearrange("p (w t) -> p w t", w=CW)
            )

        def half_sum_of_squares(rows, q, result_column):
            squares = ring.tile([P, DV], BF16, name="squares", tag="squares", bufs=2)
            nc.scalar.activation(
                out=squares[:],
                in_=rows[:, q * DV : (q + 1) * DV],
                func=ACT.Square,
                scale=0.5 ** 0.5,
                accum_out=result_column,
            )

        def transpose_X_tile(g, j):
            transpose_rows(X_raw[g], j, XT[4 * g + j][:].rearrange("p (w t) -> p w t", w=CW))
            half_sum_of_squares(X_raw[g], j, X_sq_half[:, 4 * g + j : 4 * g + j + 1])

        def transpose_kin(it, part):
            bank = new_transpose_bank()
            for pos in range(4):
                transpose_words(bank, pos, kin_raw[it], part * BANK + pos * P)
            if part == 0:
                kin_grouped[it] = ring.tile(
                    [P, NX // 2], F32, name="kin_grouped", tag="kin_grouped", bufs=3,
                    align_bytes=64,
                )
            nc.scalar.copy(
                out=kin_grouped[it][:].rearrange("p (g i u) -> p g i u", g=GROUPS, u=2)[
                    :, 2 * part : 2 * part + 2
                ],
                in_=bank[:].rearrange("p (b u i) -> p b i u", b=2, u=2),
            )
            if part == 1:
                if it + KIN_BUFS < I_TILES:
                    load_kin(it + KIN_BUFS)
                at(vector_work, now["unit"] + QUANTISE_LAG, lambda: quantise_kin(it))
                now["lam_unit"] = max(now["unit"] + LAM_LAG, now["lam_unit"] + 1)
                at(tensor_work, now["lam_unit"], lambda: lam_tile(it))

        def next_transpose_job():
            if now["job"] < len(transpose_jobs):
                job = transpose_jobs[now["job"]]
                now["job"] += 1
                job()

        def spread_query_norms(th):
            bank = new_transpose_bank()
            for q in range(4):
                tile_col = 4 * th + q
                nc.tensor.transpose(
                    out=bank[:, q * P : (q + 1) * P],
                    in_=x_sq_half[:, tile_col : tile_col + 1].to_broadcast([P, P]),
                    identity=ident[:],
                )
            nc.vector.tensor_copy(out=x_sq_half_all[:, th * BANK : (th + 1) * BANK], in_=bank[:])

        def quantise_kin(it):
            kin_codes[it] = ring.tile(
                [P, PASS], U32, name="kin_codes", tag="kin_codes", bufs=6, align_bytes=64
            )
            kin_scales[it] = ring.tile(
                [P, PASS], U8, name="kin_scales", tag="kin_scales", bufs=6, align_bytes=64
            )
            nc.vector.quantize_mx(
                out=kin_codes[it][:].bitcast(FP8X4),
                scales=kin_scales[it][:],
                in_=kin_grouped[it][:].bitcast(BF16),
            )

        def lam_tile(it):
            g, j = divmod(it, 4)
            acc = psum.tile([P, BANK], F32, name="mx", tag="mx", bufs=2)
            for c in range(GROUPS):
                nc.tensor.matmul_mx(
                    out=acc[:, 0:DY],
                    lhsT=kin_codes[it][:, c * P : (c + 1) * P].bitcast(FP8X4),
                    lhsT_scale=kin_scales[it][:, c * P : (c + 1) * P],
                    rhs=z_codes[:, c * DY : (c + 1) * DY].bitcast(FP8X4),
                    rhs_scale=z_scales[:, c * DY : (c + 1) * DY],
                    start=(c == 0),
                    stop=(c == GROUPS - 1),
                )
            if j == 0:
                lam_rows[g] = ring.tile([P, 4 * DY], BF16, name="lam_rows", tag="lam_rows", bufs=2)
            nc.scalar.copy(out=lam_rows[g][:, j * DY : (j + 1) * DY], in_=acc[:, 0:DY])
            if j == 3:
                at(vector_work, now["unit"] + 1, lambda: regroup_lam(g))
                at(vector_work, now["unit"] + 2, lambda: quantise_lam(g))

        def regroup_lam(g):
            lam_grouped[g] = ring.tile(
                [P, 4 * DY], BF16, name="lam_grouped", tag="lam_grouped", bufs=2, align_bytes=64
            )
            nc.vector.tensor_copy(
                out=lam_grouped[g][:].rearrange("p (d j) -> p d j", j=4),
                in_=lam_rows[g][:].rearrange("p (j d) -> p d j", j=4),
            )

        def quantise_lam(g):
            nc.vector.quantize_mx(
                out=lam_codes[:, g * DY : (g + 1) * DY].bitcast(FP8X4),
                scales=lam_scales[:, g * DY : (g + 1) * DY],
                in_=lam_grouped[g][:],
            )

        def kernel_values(g, th, j, gram, first, count):
            minus_half_d2 = ring.tile([P, BANK], F32, name="minus_half_d2", tag="mhd2", bufs=6)
            nc.vector.scalar_tensor_tensor(
                out=minus_half_d2[:, 0:count],
                in0=gram[:, 0:count],
                scalar=X_sq_half[:, 4 * g + j : 4 * g + j + 1],
                in1=x_sq_half_all[:, th * BANK + first : th * BANK + first + count],
                op0=ALU.subtract,
                op1=ALU.subtract,
            )
            nc.scalar.activation(
                out=k_rows[(g, th)][:, j * BANK + first : j * BANK + first + count],
                in_=minus_half_d2[:, 0:count],
                func=ACT.Exp,
                scale=1.0 / 64.0,
            )

        def regroup_k(g, th, piece):
            k_grouped[(g, th, piece)] = ring.tile(
                [P, 4 * PIECE], BF16, name="k_grouped", tag="k_grouped", bufs=2, align_bytes=64
            )
            nc.vector.tensor_scalar_min(
                out=k_grouped[(g, th, piece)][:].rearrange("p (w j) -> p w j", j=4),
                in0=k_rows[(g, th)][:].rearrange("p (j w) -> p w j", j=4)[
                    :, piece * PIECE : (piece + 1) * PIECE
                ],
                scalar1=1.0,
            )

        def quantise_k(g, th, piece):
            col = g * NT + th * BANK + piece * PIECE
            nc.vector.quantize_mx(
                out=k_codes[:, col : col + PIECE].bitcast(FP8X4),
                scales=k_scales[:, col : col + PIECE],
                in_=k_grouped[(g, th, piece)][:],
            )

        def job_slots_of(u):
            if u < 3:
                return (1, 3, 5)
            return (1, 4)

        def gram_unit(u, g, th, j, first, count):
            now["unit"] = u
            for job in tensor_work.get(u, []):
                job()
            for job in vector_work.get(u, []):
                job()
            X_pairs = XT[4 * g + j][:].bitcast(BF16).rearrange("p (w i e) -> p w i e", w=CW, e=2)
            x_pairs = xT[th][:].bitcast(BF16).rearrange("p (w t e) -> p w t e", w=CW, e=2)
            gram = psum.tile([P, BANK], F32, name="gram", tag="gram", bufs=3)
            job_slots = job_slots_of(u)
            for kc in range(UNIT_MATMULS):
                cw, e = divmod(kc, 2)
                nc.tensor.matmul(
                    out=gram[:, 0:count],
                    lhsT=X_pairs[:, cw, :, e],
                    rhs=x_pairs[:, cw, first : first + count, e],
                    start=(kc == 0),
                    stop=(kc == UNIT_MATMULS - 1),
                )
                if kc in job_slots:
                    next_transpose_job()
            if g == 0 and j == 0:
                spread_query_norms(th)
            if j == 0 and first == 0:
                k_rows[(g, th)] = ring.tile([P, 4 * BANK], BF16, name="k_rows", tag="k_rows", bufs=2)
            kernel_values(g, th, j, gram, first, count)

        def regression_passes(acc, t_tile, groups, first, last):
            t0 = t_tile * P
            for g in groups:
                nc.tensor.matmul_mx(
                    out=acc,
                    lhsT=k_codes[:, g * NT + t0 : g * NT + t0 + P].bitcast(FP8X4),
                    lhsT_scale=k_scales[:, g * NT + t0 : g * NT + t0 + P],
                    rhs=lam_codes[:, g * DY : (g + 1) * DY].bitcast(FP8X4),
                    rhs_scale=lam_scales[:, g * DY : (g + 1) * DY],
                    start=(first and g == groups[0]),
                    stop=(last and g == groups[-1]),
                )

        def finish(acc, first_tile, count):
            result = ring.tile([P, BANK], F32, name="result", tag="result", bufs=6)
            nc.vector.tensor_tensor(
                out=result[:, 0 : count * DY],
                in0=acc,
                in1=y_plus_h[:, first_tile * DY : (first_tile + count) * DY],
                op=ALU.add,
            )
            nc.sync.dma_start(
                out=out_rows[:, first_tile : first_tile + count, :],
                in_=result[:, 0 : count * DY].rearrange("p (a d) -> p a d", d=DY),
            )

        nc.vector.memset(zeros[:], 0.0)
        make_identity(nc, ident[:])
        nc.vector.memset(zero_col[:], 0.0)
        nc.scalar.activation(out=one_col[:], in_=zero_col[:], func=ACT.Exp)

        for q in range(4):
            nc.sync.dma_start(out=x_raw[:, q * DV : (q + 1) * DV], in_=x_tiles[q])
        for j in range(4):
            load_X(0, j, 1)
        nc.sync.dma_start(
            out=x_raw[:, 4 * DV : 8 * DV].rearrange("p (q c) -> p q c", q=4), in_=x_halves[1]
        )
        nc.sync.dma_start(out=z_raw[:].rearrange("p (a r) -> p a r", r=2 * DY), in_=Z_rows)
        load_X(1, 0, 4)
        for it in range(2):
            load_kin(it)
        nc.sync.dma_start(out=y_raw[:].rearrange("p (a d) -> p a d", d=DY), in_=y_rows)
        nc.sync.dma_start(out=h_raw[:].rearrange("p (a d) -> p a d", d=DY), in_=h_rows)
        for it in range(2, KIN_BUFS):
            load_kin(it)

        idle_bank = psum.tile([P, BANK], F32, name="mx", tag="mx", bufs=2)

        def idle_matmuls(count, width):
            for n in range(count):
                nc.tensor.matmul(
                    out=idle_bank[:, 0:width], lhsT=zeros[:, 0:P], rhs=zeros[:, 0:width],
                    start=True, stop=True,
                )

        idle_matmuls(4, BANK)

        def transpose_x_tile(q):
            h, q4 = divmod(q, 4)
            transpose_rows(
                x_raw, q,
                xT[h][:].rearrange("p (w t) -> p w t", w=CW)[:, :, q4 * P : (q4 + 1) * P],
            )
            half_sum_of_squares(x_raw, q, x_sq_half[:, q : q + 1])

        for q in range(4):
            transpose_x_tile(q)
            idle_matmuls(1, BANK // 2)
        transpose_X_tile(0, 0)
        idle_matmuls(1, BANK)

        for j in range(1, 4):
            transpose_jobs.append(lambda j=j: transpose_X_tile(0, j))

        for q in range(4, T_TILES):
            transpose_jobs.append(lambda q=q: transpose_x_tile(q))
        kin_halves = [(it, part) for it in range(I_TILES) for part in range(2)]
        taken = 0
        for u in range(3, UNITS):
            g, j = (u + X_LEAD) // 8, (u + X_LEAD) % 8
            places = len(job_slots_of(u))
            if g < GROUPS and j < 4:
                transpose_jobs.append(lambda g=g, j=j: transpose_X_tile(g, j))
                places -= 1
            for n in range(places):
                if u >= KIN_FIRST_UNIT and taken < len(kin_halves):
                    it, part = kin_halves[taken]
                    transpose_jobs.append(lambda it=it, part=part: transpose_kin(it, part))
                    taken += 1
                else:
                    transpose_jobs.append(lambda: None)
        assert taken == len(kin_halves)

        z_by_column = z_raw[:].rearrange("p (g t d) -> p g d t", g=GROUPS, t=4)
        z_words = z_grouped[:].rearrange("p (g d t) -> p g d t", g=GROUPS, t=4)
        for g in range(GROUPS):
            nc.gpsimd.tensor_scalar(
                out=z_words[:, g], in0=z_by_column[:, g], scalar1=1.0, scalar2=0.0,
                op0=ALU.mult, op1=ALU.add,
            )
        for pair in range(T_TILES // 2):
            cols = slice(pair * BANK, (pair + 1) * BANK)
            nc.gpsimd.tensor_tensor(
                out=y_plus_h[:, cols], in0=y_raw[:, cols], in1=h_raw[:, cols], op=ALU.add
            )
        at(
            vector_work, Z_UNIT,
            lambda: nc.vector.quantize_mx(
                out=z_codes[:].bitcast(FP8X4), scales=z_scales[:], in_=z_grouped[:]
            ),
        )

        last_g, last_th = GROUPS - 1, HALVES - 1
        units = []
        for g in range(GROUPS):
            for th in range(HALVES):
                widths = [PIECE, PIECE] if (g, th) == (last_g, last_th) else [BANK]
                for n, count in enumerate(widths):
                    for j in range(4):
                        units.append((g, th, j, n * count, count))
        for u, (g, th, j, first, count) in enumerate(units):
            if u % 8 == 2 and g + 2 < GROUPS:
                load_X(g + 2, 0, 4)
            gram_unit(u, g, th, j, first, count)
            if j == 3 and count == BANK:
                step = 2 if (g, th) == (last_g, last_th - 1) else 1
                start = u + 1 if step == 2 else u + 2
                at(vector_work, start + step, lambda g=g, th=th: regroup_k(g, th, 0))
                at(vector_work, start + 2 * step, lambda g=g, th=th: quantise_k(g, th, 0))
                at(vector_work, start + 2 * step, lambda g=g, th=th: regroup_k(g, th, 1))
                at(vector_work, start + 3 * step, lambda g=g, th=th: quantise_k(g, th, 1))
            if j == 3 and count == PIECE and first == 0:
                at(vector_work, u + 2, lambda: regroup_k(last_g, last_th, 0))
                at(vector_work, u + 4, lambda: quantise_k(last_g, last_th, 0))

        assert max(vector_work) < len(units) and max(tensor_work) < len(units)
        assert now["job"] >= len(transpose_jobs) - 2 * (len(units) - UNITS)

        regroup_k(last_g, last_th, 1)
        quantise_k(last_g, last_th, 1)
        all_groups = list(range(GROUPS))
        for pair in range(T_TILES // 2 - 1):
            acc = (
                psum.tile([P, BANK], F32, name="mx", tag="mx", bufs=2)
                if pair % 2 == 0
                else new_transpose_bank()
            )
            for s in range(2):
                regression_passes(acc[:, s * DY : (s + 1) * DY], 2 * pair + s, all_groups, True, True)
            finish(acc[:], 2 * pair, 2)
        for t_tile in range(T_TILES - 2, T_TILES):
            acc = new_transpose_bank()
            regression_passes(acc[:, 0:DY], t_tile, all_groups, True, True)
            finish(acc[:, 0:DY], t_tile, 1)
